import numpy as np
import ml_dtypes


def mxq(x, axis, fmt="e4m3"):
    dtype, down = {"e4m3": (ml_dtypes.float8_e4m3fn, 7), "e5m2": (ml_dtypes.float8_e5m2, 14)}[fmt]
    v = np.moveaxis(np.asarray(x, np.float32).astype(ml_dtypes.bfloat16).astype(np.float64), axis, -1)
    blocks = v.reshape(v.shape[:-1] + (-1, 32))
    amax = np.abs(blocks).max(-1, keepdims=True)
    byte = np.maximum(np.where(amax > 0, np.frexp(amax)[1] - 1 + 127, 0) - down, 1)
    scale = np.exp2(byte - 127.0)
    codes = (blocks / scale).astype(np.float32).astype(dtype).astype(np.float64)
    return np.moveaxis((codes * scale).reshape(v.shape), -1, axis)


WIDE = False


def mx_kscale(k):
    if not WIDE:
        return np.ones(k)
    levels = np.array([10, -10, 5, -5, 0])
    a = np.random.permutation(np.resize(levels, k // 512 * 4)).reshape(k // 512, 4)
    idx = np.arange(k)
    return np.exp2(a[idx // 512, idx % 128 // 32])


BF16 = ml_dtypes.bfloat16


def bf(x):
    return np.asarray(x, np.float32).astype(BF16)


def f64(x):
    return np.asarray(x).astype(np.float64)


B, C, O, H, W, KT = 2, 512, 512, 32, 40, 7

OFFSETS = ((0, 0), (-1, 0), (1, 0), (0, -1), (0, 1))


def setup_inputs():
    s = mx_kscale(C)
    return {"x": bf(np.random.standard_normal((B, C, H, W)) * s[None, :, None, None]),
            "w": bf(np.random.standard_normal((len(OFFSETS), C, KT, KT)) * 2.0 / s[None, :, None, None]),
            "conv_w": bf(np.random.standard_normal((O, C)) / np.sqrt(C) / s[None, :]),
            "conv_b": bf(np.random.standard_normal(O) * 0.3)}


def reference(x, w, conv_w, conv_b):
    x, w, conv_w, conv_b = f64(x), f64(w), f64(conv_w), f64(conv_b)
    nb_, nc_, hh, ww = x.shape
    k = w.shape[-1]
    ph = k - hh % k
    pw = k - ww % k
    xpd = np.pad(x, ((0, 0), (0, 0), (0, ph), (0, pw)))
    hp, wp = hh + ph, ww + pw
    wpos = np.tile(w, (1, 1, hp // k, wp // k))
    xh = np.pad(xpd, ((0, 0), (0, 0), (1, 1), (1, 1)))
    att = np.zeros_like(xpd)
    for n, (dh, dw) in enumerate(OFFSETS):
        nb = xh[:, :, 1 + dh:1 + dh + hp, 1 + dw:1 + dw + wp]
        att = att + wpos[n][None] * nb
    e = np.exp(att - att.max(axis=1, keepdims=True))
    att = e / e.sum(axis=1, keepdims=True)
    x1 = xpd * att + xpd
    x1 = x1[:, :, :hh, :ww]
    y = np.matmul(mxq(conv_w, 1, "e4m3"), mxq(x1, 1, "e4m3").reshape(nb_, nc_, hh * ww))
    return y.reshape(nb_, -1, hh, ww) + conv_b[None, :, None, None]

@@ -1,0 +1,268 @@
+from contextlib import ExitStack
+
+import concourse.mybir as mybir
+from concourse.masks import make_identity
+
+BF16 = mybir.dt.bfloat16
+F32 = mybir.dt.float32
+I32 = mybir.dt.int32
+U32 = mybir.dt.uint32
+U8 = mybir.dt.uint8
+FP8X4 = mybir.dt.float8_e4m3fn_x4
+ALU = mybir.AluOpType
+ACT = mybir.ActivationFunctionType
+AXIS = mybir.AxisListType
+
+P = 128
+B, C, O, H, W, KT = 2, 512, 512, 32, 40, 7
+CB = C // P
+OB = O // P
+IMG = H * W
+KCOLS = (W + KT - 1) // KT
+WPAD = KCOLS * KT
+MX_N = 512
+ALIGN = 64
+
+OFFSETS = ((0, 0), (-1, 0), (1, 0), (0, -1), (0, 1))
+CENTRE = 0
+VECTOR_TAPS = (3, 4, 1, 2)
+
+FLOPS = 2 * B * IMG * C * O
+
+
+def rows_of(r):
+    return (H - r + KT - 1) // KT
+
+
+def class_size(r):
+    return B * rows_of(r) * KCOLS
+
+
+def group_start(r):
+    return sum(KT * class_size(rr) for rr in range(r))
+
+
+def class_start(r, q):
+    return group_start(r) + q * class_size(r)
+
+
+NPOS = B * H * WPAD
+XROOM = (H + KT - 1) * W
+
+
+def tile_lablock_kernel(tc, x, w, conv_w, conv_b, out):
+    nc = tc.nc
+    with ExitStack() as ctx:
+        keep = ctx.enter_context(tc.tile_pool(name="keep", bufs=1))
+        work = ctx.enter_context(tc.tile_pool(name="work", bufs=3))
+        small = ctx.enter_context(tc.tile_pool(name="small", bufs=4))
+        stores = ctx.enter_context(tc.tile_pool(name="stores", bufs=6))
+        psum_setup = ctx.enter_context(tc.psum_pool(name="psum_setup", bufs=1))
+        psum_turn = ctx.enter_context(tc.psum_pool(name="psum_turn", bufs=2))
+        psum_conv = ctx.enter_context(tc.psum_pool(name="psum_conv", bufs=3))
+
+        x_img = keep.tile([P, CB, B, XROOM], BF16)
+        for t in range(CB):
+            nc.sync.dma_start(
+                out=x_img[:, t, :, 0:IMG],
+                in_=x[:, t * P : (t + 1) * P].rearrange("b p i j -> p b (i j)"),
+            )
+        w_bf = keep.tile([P, len(OFFSETS) * CB, KT * KT], BF16)
+        nc.scalar.dma_start(out=w_bf[:], in_=w.rearrange("n (t p) r q -> p (n t) (r q)", p=P))
+        cw_rows = keep.tile([P, OB, C], BF16)
+        nc.scalar.dma_start(out=cw_rows[:], in_=conv_w.rearrange("(ob p) c -> p ob c", p=P))
+        bias_rows = keep.tile([P, P], BF16)
+        nc.vector.memset(bias_rows[:], 0.0)
+        nc.scalar.dma_start(out=bias_rows[0:OB, :], in_=conv_b.rearrange("(ob p) -> ob p", p=P))
+
+        ident_f32 = keep.tile([P, P], F32)
+        make_identity(nc, ident_f32[:])
+        ident_bf = keep.tile([P, P], BF16)
+        make_identity(nc, ident_bf[:])
+
+        x_cls = keep.tile([P, CB, NPOS], BF16)
+        nc.vector.memset(x_cls[:].bitcast(I32), 0)
+
+        w_f32 = keep.tile([P, len(OFFSETS) * CB, KT * KT], F32)
+        nc.vector.tensor_copy(out=w_f32[:], in_=w_bf[:])
+
+        cw_grouped = keep.tile([P, O, CB], BF16, align_bytes=64)
+        for ob in range(OB):
+            cw_turned = psum_setup.tile([P, CB, P], BF16, tag="setup")
+            for t in range(CB):
+                nc.tensor.transpose(cw_turned[:, t, :], cw_rows[:, ob, t * P : (t + 1) * P], ident_bf[:])
+            nc.vector.tensor_copy(
+                out=cw_grouped[:, ob * P : (ob + 1) * P, :],
+                in_=cw_turned[:].rearrange("p t o -> p o t"),
+            )
+        cw_codes = keep.tile([P, O], U32, align_bytes=64)
+        cw_scales = keep.tile([P, O], U8, align_bytes=64)
+        nc.vector.quantize_mx(
+            out=cw_codes[:].bitcast(FP8X4),
+            scales=cw_scales[:],
+            in_=cw_grouped[:].rearrange("p o t -> p (o t)"),
+        )
+
+        bias_turned = psum_setup.tile([P, CB, P], BF16, tag="setup")
+        nc.tensor.transpose(bias_turned[:, 0, :], bias_rows[:], ident_bf[:])
+        bias = keep.tile([P, OB], F32)
+        nc.vector.tensor_copy(out=bias[:], in_=bias_turned[:, 0, 0:OB])
+
+        for t in range(CB):
+            for r in range(KT):
+                na = rows_of(r)
+                for b in range(B):
+                    src = (
+                        x_img[:, t, b, r * W : r * W + KT * W * na]
+                        .rearrange("p (a z) -> p a z", z=KT * W)[:, :, 0:WPAD]
+                        .rearrange("p a (k q) -> p q a k", q=KT)
+                    )
+                    dst = x_cls[:, t, group_start(r) : group_start(r + 1)].rearrange(
+                        "p (q b a k) -> p q b a k", q=KT, b=B, a=na
+                    )[:, :, b]
+                    full_q = W - (KCOLS - 1) * KT
+                    pieces = (
+                        (dst[:, 0:full_q], src[:, 0:full_q]),
+                        (dst[:, full_q:KT, :, 0 : KCOLS - 1], src[:, full_q:KT, :, 0 : KCOLS - 1]),
+                    )
+                    for piece_out, piece_in in pieces:
+                        if t % 2 == 0:
+                            nc.vector.tensor_copy(out=piece_out, in_=piece_in)
+                        else:
+                            nc.scalar.copy(out=piece_out, in_=piece_in)
+
+        logits = keep.tile([P, CB, NPOS], F32)
+        x1_grouped = keep.tile([P, NPOS, CB], BF16, align_bytes=64)
+        x1_codes = keep.tile([P, NPOS], U32, align_bytes=64)
+        x1_scales = keep.tile([P, NPOS], U8, align_bytes=64)
+
+        def stencil(r):
+            na = rows_of(r)
+            size = class_size(r)
+            centre = work.tile([P, CB, KT * class_size(0)], F32, tag="centre")
+            for t in range(CB):
+                for q in range(KT):
+                    nc.scalar.activation(
+                        out=centre[:, t, q * size : (q + 1) * size],
+                        in_=x_cls[:, t, class_start(r, q) : class_start(r, q) + size],
+                        func=ACT.Copy,
+                        scale=w_f32[:, CENTRE * CB + t, r * KT + q : r * KT + q + 1],
+                    )
+            for tap in VECTOR_TAPS:
+                di, dj = OFFSETS[tap]
+                r2, a_shift = (r + di) % KT, (r + di) // KT
+                na2 = rows_of(r2)
+                a_lo = max(0, -a_shift)
+                a_cnt = min(na, na2 - a_shift) - a_lo
+                for t in range(CB):
+                    for q in range(KT):
+                        q2, k_shift = (q + dj) % KT, (q + dj) // KT
+                        start = class_start(r, q)
+                        start2 = class_start(r2, q2) + k_shift
+                        acc = logits[:, t, start : start + size].rearrange("p (b z) -> p b z", b=B)[
+                            :, :, a_lo * KCOLS : (a_lo + a_cnt) * KCOLS
+                        ]
+                        moved = x_cls[:, t, start2 : start2 + class_size(r2)].rearrange(
+                            "p (b z) -> p b z", b=B
+                        )[:, :, (a_lo + a_shift) * KCOLS : (a_lo + a_shift + a_cnt) * KCOLS]
+                        if tap == VECTOR_TAPS[0]:
+                            before = centre[:, t, q * size : (q + 1) * size].rearrange("p (b z) -> p b z", b=B)
+                        else:
+                            before = acc
+                        nc.vector.scalar_tensor_tensor(
+                            out=acc,
+                            in0=moved,
+                            scalar=w_f32[:, tap * CB + t, r * KT + q : r * KT + q + 1],
+                            in1=before,
+                            op0=ALU.mult,
+                            op1=ALU.add,
+                        )
+
+        def attend(tile_index):
+            cols = slice(tile_index * P, (tile_index + 1) * P)
+            logits_t = psum_turn.tile([P, CB, P], F32, tag="logits_t")
+            for t in range(CB):
+                nc.tensor.transpose(logits_t[:, t, :], logits[:, t, cols], ident_f32[:])
+            neg_max = small.tile([P, 1], F32, tag="neg_max")
+            nc.vector.tensor_reduce(
+                out=neg_max[:],
+                in_=logits_t[:].rearrange("p t c -> p (t c)"),
+                axis=AXIS.X,
+                op=ALU.max,
+                negate=True,
+            )
+            gain = work.tile([P, C], F32, tag="gain")
+            total = small.tile([P, 1], F32, tag="total")
+            nc.scalar.activation(
+                out=gain[:],
+                in_=logits_t[:].rearrange("p t c -> p (t c)"),
+                func=ACT.Exp,
+                bias=neg_max[:, 0:1],
+                scale=1.0,
+                accum_out=total[:, 0:1],
+            )
+            inv_total = small.tile([P, 1], F32, tag="inv_total")
+            nc.vector.reciprocal(inv_total[:], total[:])
+            nc.scalar.activation(
+                out=gain[:], in_=gain[:], func=ACT.Identity, bias=1.0, scale=inv_total[:, 0:1]
+            )
+            gain_c = psum_turn.tile([P, CB, P], F32, tag="gain_c")
+            for t in range(CB):
+                nc.tensor.transpose(gain_c[:, t, :], gain[:, t * P : (t + 1) * P], ident_f32[:])
+            nc.vector.tensor_tensor(
+                out=x1_grouped[:, cols, :],
+                in0=gain_c[:].rearrange("p t s -> p s t"),
+                in1=x_cls[:, :, cols].rearrange("p t s -> p s t"),
+                op=ALU.mult,
+            )
+            nc.vector.quantize_mx(
+                out=x1_codes[:, cols].bitcast(FP8X4),
+                scales=x1_scales[:, cols],
+                in_=x1_grouped[:, cols, :].rearrange("p s t -> p (s t)"),
+            )
+
+        def window_start(r):
+            end = -(-group_start(r + 1) // ALIGN) * ALIGN
+            return max(0, end - MX_N)
+
+        def convolve(r):
+            na = rows_of(r)
+            first = window_start(r)
+            inside = group_start(r) - first
+            for ob in range(OB):
+                conv = psum_conv.tile([P, MX_N], F32, tag="conv")
+                nc.tensor.matmul_mx(
+                    out=conv[:],
+                    lhsT=cw_codes[:, ob * P : (ob + 1) * P].bitcast(FP8X4),
+                    lhsT_scale=cw_scales[:, ob * P : (ob + 1) * P],
+                    rhs=x1_codes[:, first : first + MX_N].bitcast(FP8X4),
+                    rhs_scale=x1_scales[:, first : first + MX_N],
+                    start=True,
+                    stop=True,
+                )
+                by_class = conv[:, inside : inside + KT * class_size(r)].rearrange(
+                    "p (q b a k) -> p b a k q", q=KT, b=B, a=na
+                )
+                for b in range(B):
+                    rows = stores.tile([P, rows_of(0), WPAD], F32, tag="rows")
+                    nc.scalar.activation(
+                        out=rows[:, 0:na, :].rearrange("p a (k q) -> p a k q", q=KT),
+                        in_=by_class[:, b],
+                        func=ACT.Identity,
+                        bias=bias[:, ob : ob + 1],
+                        scale=1.0,
+                    )
+                    nc.sync.dma_start(
+                        out=out[b, ob * P : (ob + 1) * P, r:H:KT, :], in_=rows[:, 0:na, 0:W]
+                    )
+
+        tiles_done = 0
+        groups_done = 0
+        for r in range(KT):
+            stencil(r)
+            while (tiles_done + 1) * P <= group_start(r + 1):
+                attend(tiles_done)
+                tiles_done += 1
+            while groups_done <= r and window_start(groups_done) + MX_N <= tiles_done * P:
+                convolve(groups_done)
+                groups_done += 1

@@ -25,7 +25,8 @@ ALIGN = 64
 
 OFFSETS = ((0, 0), (-1, 0), (1, 0), (0, -1), (0, 1))
 CENTRE = 0
-VECTOR_TAPS = (3, 4, 1, 2)
+SIDE = 4
+VECTOR_TAPS = (3, 1, 2)
 
 FLOPS = 2 * B * IMG * C * O
 
@@ -47,6 +48,8 @@ def class_start(r, q):
 
 
 NPOS = B * H * WPAD
+NTILES = NPOS // P
+MAX_CLASSES = 3
 XROOM = (H + KT - 1) * W
 
 
@@ -131,42 +134,70 @@ def tile_lablock_kernel(tc, x, w, conv_w, conv_b, out):
                         else:
                             nc.scalar.copy(out=piece_out, in_=piece_in)
 
-        logits = keep.tile([P, CB, NPOS], F32)
+        main = keep.tile([P, CB, NPOS], F32)
+        side = keep.tile([P, CB, NPOS], F32)
         x1_grouped = keep.tile([P, NPOS, CB], BF16, align_bytes=64)
         x1_codes = keep.tile([P, NPOS], U32, align_bytes=64)
         x1_scales = keep.tile([P, NPOS], U8, align_bytes=64)
 
-        def stencil(r):
-            na = rows_of(r)
-            size = class_size(r)
-            centre = work.tile([P, CB, KT * class_size(0)], F32, tag="centre")
-            for t in range(CB):
-                for q in range(KT):
+        centre_of = {}
+        logits_t_of = {}
+        neg_max_of = {}
+        gain_of = {}
+        total_of = {}
+        inv_total_of = {}
+        gain_c_of = {}
+
+        def classes_of(index):
+            return [
+                (r, q)
+                for r in range(KT)
+                for q in range(KT)
+                if index * P <= class_start(r, q) < (index + 1) * P
+            ]
+
+        def multiply_on_scalar(index):
+            centre = work.tile([P, MAX_CLASSES, CB, class_size(0)], F32, tag="centre")
+            for slot, (r, q) in enumerate(classes_of(index)):
+                size = class_size(r)
+                start = class_start(r, q)
+                start2 = class_start(r, (q + 1) % KT) + (q + 1) // KT
+                for t in range(CB):
                     nc.scalar.activation(
-                        out=centre[:, t, q * size : (q + 1) * size],
-                        in_=x_cls[:, t, class_start(r, q) : class_start(r, q) + size],
+                        out=centre[:, slot, t, 0:size],
+                        in_=x_cls[:, t, start : start + size],
                         func=ACT.Copy,
                         scale=w_f32[:, CENTRE * CB + t, r * KT + q : r * KT + q + 1],
                     )
+                    nc.scalar.activation(
+                        out=side[:, t, start : start + size],
+                        in_=x_cls[:, t, start2 : start2 + size],
+                        func=ACT.Copy,
+                        scale=w_f32[:, SIDE * CB + t, r * KT + q : r * KT + q + 1],
+                    )
+            centre_of[index] = centre
+
+        def add_taps(index):
+            centre = centre_of[index]
             for tap in VECTOR_TAPS:
                 di, dj = OFFSETS[tap]
-                r2, a_shift = (r + di) % KT, (r + di) // KT
-                na2 = rows_of(r2)
-                a_lo = max(0, -a_shift)
-                a_cnt = min(na, na2 - a_shift) - a_lo
-                for t in range(CB):
-                    for q in range(KT):
-                        q2, k_shift = (q + dj) % KT, (q + dj) // KT
-                        start = class_start(r, q)
-                        start2 = class_start(r2, q2) + k_shift
-                        acc = logits[:, t, start : start + size].rearrange("p (b z) -> p b z", b=B)[
+                for slot, (r, q) in enumerate(classes_of(index)):
+                    size = class_size(r)
+                    r2, a_shift = (r + di) % KT, (r + di) // KT
+                    q2, k_shift = (q + dj) % KT, (q + dj) // KT
+                    a_lo = max(0, -a_shift)
+                    a_cnt = min(rows_of(r), rows_of(r2) - a_shift) - a_lo
+                    start = class_start(r, q)
+                    start2 = class_start(r2, q2) + k_shift
+                    for t in range(CB):
+                        acc = main[:, t, start : start + size].rearrange("p (b z) -> p b z", b=B)[
                             :, :, a_lo * KCOLS : (a_lo + a_cnt) * KCOLS
                         ]
                         moved = x_cls[:, t, start2 : start2 + class_size(r2)].rearrange(
                             "p (b z) -> p b z", b=B
                         )[:, :, (a_lo + a_shift) * KCOLS : (a_lo + a_shift + a_cnt) * KCOLS]
                         if tap == VECTOR_TAPS[0]:
-                            before = centre[:, t, q * size : (q + 1) * size].rearrange("p (b z) -> p b z", b=B)
+                            before = centre[:, slot, t, 0:size].rearrange("p (b z) -> p b z", b=B)
                         else:
                             before = acc
                         nc.vector.scalar_tensor_tensor(
@@ -178,40 +209,67 @@ def tile_lablock_kernel(tc, x, w, conv_w, conv_b, out):
                             op1=ALU.add,
                         )
 
-        def attend(tile_index):
-            cols = slice(tile_index * P, (tile_index + 1) * P)
+        def turn_logits(index):
+            cols = slice(index * P, (index + 1) * P)
             logits_t = psum_turn.tile([P, CB, P], F32, tag="logits_t")
             for t in range(CB):
-                nc.tensor.transpose(logits_t[:, t, :], logits[:, t, cols], ident_f32[:])
+                nc.tensor.matmul(
+                    out=logits_t[:, t, :], lhsT=main[:, t, cols], rhs=ident_f32[:],
+                    is_transpose=True, start=True, stop=False,
+                )
+                nc.tensor.matmul(
+                    out=logits_t[:, t, :], lhsT=side[:, t, cols], rhs=ident_f32[:],
+                    is_transpose=True, start=False, stop=True,
+                )
+            logits_t_of[index] = logits_t
+
+        def find_max(index):
             neg_max = small.tile([P, 1], F32, tag="neg_max")
             nc.vector.tensor_reduce(
                 out=neg_max[:],
-                in_=logits_t[:].rearrange("p t c -> p (t c)"),
+                in_=logits_t_of[index][:].rearrange("p t c -> p (t c)"),
                 axis=AXIS.X,
                 op=ALU.max,
                 negate=True,
             )
+            neg_max_of[index] = neg_max
+
+        def exponentials(index):
             gain = work.tile([P, C], F32, tag="gain")
             total = small.tile([P, 1], F32, tag="total")
             nc.scalar.activation(
                 out=gain[:],
-                in_=logits_t[:].rearrange("p t c -> p (t c)"),
+                in_=logits_t_of[index][:].rearrange("p t c -> p (t c)"),
                 func=ACT.Exp,
-                bias=neg_max[:, 0:1],
+                bias=neg_max_of[index][:, 0:1],
                 scale=1.0,
                 accum_out=total[:, 0:1],
             )
+            gain_of[index] = gain
+            total_of[index] = total
+
+        def invert_total(index):
             inv_total = small.tile([P, 1], F32, tag="inv_total")
-            nc.vector.reciprocal(inv_total[:], total[:])
+            nc.vector.reciprocal(inv_total[:], total_of[index][:])
+            inv_total_of[index] = inv_total
+
+        def make_gain(index):
+            gain = gain_of[index]
             nc.scalar.activation(
-                out=gain[:], in_=gain[:], func=ACT.Identity, bias=1.0, scale=inv_total[:, 0:1]
+                out=gain[:], in_=gain[:], func=ACT.Identity, bias=1.0, scale=inv_total_of[index][:, 0:1]
             )
+
+        def turn_gain(index):
             gain_c = psum_turn.tile([P, CB, P], F32, tag="gain_c")
             for t in range(CB):
-                nc.tensor.transpose(gain_c[:, t, :], gain[:, t * P : (t + 1) * P], ident_f32[:])
+                nc.tensor.transpose(gain_c[:, t, :], gain_of[index][:, t * P : (t + 1) * P], ident_f32[:])
+            gain_c_of[index] = gain_c
+
+        def make_x1(index):
+            cols = slice(index * P, (index + 1) * P)
             nc.vector.tensor_tensor(
                 out=x1_grouped[:, cols, :],
-                in0=gain_c[:].rearrange("p t s -> p s t"),
+                in0=gain_c_of[index][:].rearrange("p t s -> p s t"),
                 in1=x_cls[:, :, cols].rearrange("p t s -> p s t"),
                 op=ALU.mult,
             )
@@ -225,7 +283,7 @@ def tile_lablock_kernel(tc, x, w, conv_w, conv_b, out):
             end = -(-group_start(r + 1) // ALIGN) * ALIGN
             return max(0, end - MX_N)
 
-        def convolve(r):
+        def convolve(r, vector_helps):
             na = rows_of(r)
             first = window_start(r)
             inside = group_start(r) - first
@@ -245,24 +303,47 @@ def tile_lablock_kernel(tc, x, w, conv_w, conv_b, out):
                 )
                 for b in range(B):
                     rows = stores.tile([P, rows_of(0), WPAD], F32, tag="rows")
-                    nc.scalar.activation(
-                        out=rows[:, 0:na, :].rearrange("p a (k q) -> p a k q", q=KT),
-                        in_=by_class[:, b],
-                        func=ACT.Identity,
-                        bias=bias[:, ob : ob + 1],
-                        scale=1.0,
-                    )
+                    in_order = rows[:, 0:na, :].rearrange("p a (k q) -> p a k q", q=KT)
+                    if vector_helps and ob % 2 == 1:
+                        nc.vector.tensor_scalar(
+                            out=in_order,
+                            in0=by_class[:, b],
+                            scalar1=bias[:, ob : ob + 1],
+                            scalar2=None,
+                            op0=ALU.add,
+                        )
+                    else:
+                        nc.scalar.activation(
+                            out=in_order,
+                            in_=by_class[:, b],
+                            func=ACT.Identity,
+                            bias=bias[:, ob : ob + 1],
+                            scale=1.0,
+                        )
                     nc.sync.dma_start(
                         out=out[b, ob * P : (ob + 1) * P, r:H:KT, :], in_=rows[:, 0:na, 0:W]
                     )
 
-        tiles_done = 0
+        def running(index):
+            return 0 <= index < NTILES
+
         groups_done = 0
-        for r in range(KT):
-            stencil(r)
-            while (tiles_done + 1) * P <= group_start(r + 1):
-                attend(tiles_done)
-                tiles_done += 1
-            while groups_done <= r and window_start(groups_done) + MX_N <= tiles_done * P:
-                convolve(groups_done)
+        multiply_on_scalar(0)
+        for step in range(NTILES + 3):
+            if running(step + 1):
+                multiply_on_scalar(step + 1)
+            if running(step):
+                add_taps(step)
+                turn_logits(step)
+            if running(step - 1):
+                find_max(step - 1)
+                exponentials(step - 1)
+            if running(step - 2):
+                invert_total(step - 2)
+                make_gain(step - 2)
+                turn_gain(step - 2)
+            if running(step - 3):
+                make_x1(step - 3)
+            while groups_done < KT and window_start(groups_done) + MX_N <= (step - 2) * P:
+                convolve(groups_done, vector_helps=step >= NTILES)
                 groups_done += 1

@@ -255,8 +255,13 @@ def tile_lablock_kernel(tc, x, w, conv_w, conv_b, out):
 
         def make_gain(index):
             gain = gain_of[index]
-            nc.scalar.activation(
-                out=gain[:], in_=gain[:], func=ACT.Identity, bias=1.0, scale=inv_total_of[index][:, 0:1]
+            nc.vector.tensor_scalar(
+                out=gain[:],
+                in0=gain[:],
+                scalar1=inv_total_of[index][:, 0:1],
+                scalar2=1.0,
+                op0=ALU.mult,
+                op1=ALU.add,
             )
 
         def turn_gain(index):

@@ -20,12 +20,18 @@ OB = O // P
 IMG = H * W
 KCOLS = (W + KT - 1) // KT
 WPAD = KCOLS * KT
+ROW = B * KCOLS
+NPOS = H * KT * ROW
+NTILES = NPOS // P
+SRC_ROWS = (H + KT - 1) // KT + 2
+SRC_CLASS = SRC_ROWS * ROW
+SRC_COLS = -(-KT * KT * SRC_CLASS // 16) * 16
+XROOM = (H + KT - 1) * W
 MX_N = 512
 ALIGN = 64
 
 OFFSETS = ((0, 0), (-1, 0), (1, 0), (0, -1), (0, 1))
-CENTRE = 0
-SIDE = 4
+SCALAR_TAPS = (0, 4)
 VECTOR_TAPS = (3, 1, 2)
 
 FLOPS = 2 * B * IMG * C * O
@@ -36,7 +42,7 @@ def rows_of(r):
 
 
 def class_size(r):
-    return B * rows_of(r) * KCOLS
+    return rows_of(r) * ROW
 
 
 def group_start(r):
@@ -47,10 +53,33 @@ def class_start(r, q):
     return group_start(r) + q * class_size(r)
 
 
-NPOS = B * H * WPAD
-NTILES = NPOS // P
-MAX_CLASSES = 3
-XROOM = (H + KT - 1) * W
+def source_start(r, q, tap):
+    di, dj = OFFSETS[tap]
+    r2, a_shift = (r + di) % KT, (r + di) // KT
+    q2, k_shift = (q + dj) % KT, (q + dj) // KT
+    return (r2 * KT + q2) * SRC_CLASS + (1 + a_shift) * ROW + k_shift
+
+
+def classes_of(index):
+    return [
+        (r, q) for r in range(KT) for q in range(KT) if index * P <= class_start(r, q) < (index + 1) * P
+    ]
+
+
+def pieces_of(index):
+    pieces = []
+    for r in range(KT):
+        for q in range(KT):
+            lo = max(class_start(r, q), index * P)
+            hi = min(class_start(r, q) + class_size(r), (index + 1) * P)
+            if lo < hi:
+                pieces.append((r, q, lo - class_start(r, q), hi - lo))
+    return pieces
+
+
+def window_start(r):
+    end = -(-group_start(r + 1) // ALIGN) * ALIGN
+    return max(0, end - MX_N)
 
 
 def tile_lablock_kernel(tc, x, w, conv_w, conv_b, out):
@@ -83,8 +112,30 @@ def tile_lablock_kernel(tc, x, w, conv_w, conv_b, out):
         ident_bf = keep.tile([P, P], BF16)
         make_identity(nc, ident_bf[:])
 
-        x_cls = keep.tile([P, CB, NPOS], BF16)
-        nc.vector.memset(x_cls[:].bitcast(I32), 0)
+        x_cls = keep.tile([P, CB, SRC_COLS], BF16)
+        full_q = W - (KCOLS - 1) * KT
+        for t in range(CB):
+            nc.vector.memset(x_cls[:, t, :].bitcast(I32), 0)
+            for r in range(KT):
+                na = rows_of(r)
+                for b in range(B):
+                    src = (
+                        x_img[:, t, b, r * W : r * W + KT * W * na]
+                        .rearrange("p (a z) -> p a z", z=KT * W)[:, :, 0:WPAD]
+                        .rearrange("p a (k q) -> p q a k", q=KT)
+                    )
+                    dst = x_cls[:, t, r * KT * SRC_CLASS : (r + 1) * KT * SRC_CLASS].rearrange(
+                        "p (q a b k) -> p q a b k", q=KT, a=SRC_ROWS, b=B
+                    )[:, :, 1 : 1 + na, b, :]
+                    pieces = (
+                        (dst[:, 0:full_q], src[:, 0:full_q]),
+                        (dst[:, full_q:KT, :, 0 : KCOLS - 1], src[:, full_q:KT, :, 0 : KCOLS - 1]),
+                    )
+                    for piece_out, piece_in in pieces:
+                        if t % 2 == 0:
+                            nc.vector.tensor_copy(out=piece_out, in_=piece_in)
+                        else:
+                            nc.scalar.copy(out=piece_out, in_=piece_in)
 
         w_f32 = keep.tile([P, len(OFFSETS) * CB, KT * KT], F32)
         nc.vector.tensor_copy(out=w_f32[:], in_=w_bf[:])
@@ -111,36 +162,11 @@ def tile_lablock_kernel(tc, x, w, conv_w, conv_b, out):
         bias = keep.tile([P, OB], F32)
         nc.vector.tensor_copy(out=bias[:], in_=bias_turned[:, 0, 0:OB])
 
-        for t in range(CB):
-            for r in range(KT):
-                na = rows_of(r)
-                for b in range(B):
-                    src = (
-                        x_img[:, t, b, r * W : r * W + KT * W * na]
-                        .rearrange("p (a z) -> p a z", z=KT * W)[:, :, 0:WPAD]
-                        .rearrange("p a (k q) -> p q a k", q=KT)
-                    )
-                    dst = x_cls[:, t, group_start(r) : group_start(r + 1)].rearrange(
-                        "p (q b a k) -> p q b a k", q=KT, b=B, a=na
-                    )[:, :, b]
-                    full_q = W - (KCOLS - 1) * KT
-                    pieces = (
-                        (dst[:, 0:full_q], src[:, 0:full_q]),
-                        (dst[:, full_q:KT, :, 0 : KCOLS - 1], src[:, full_q:KT, :, 0 : KCOLS - 1]),
-                    )
-                    for piece_out, piece_in in pieces:
-                        if t % 2 == 0:
-                            nc.vector.tensor_copy(out=piece_out, in_=piece_in)
-                        else:
-                            nc.scalar.copy(out=piece_out, in_=piece_in)
-
-        main = keep.tile([P, CB, NPOS], F32)
-        side = keep.tile([P, CB, NPOS], F32)
-        x1_grouped = keep.tile([P, NPOS, CB], BF16, align_bytes=64)
+        scalar_products = keep.tile([P, len(SCALAR_TAPS), CB, NPOS], F32)
         x1_codes = keep.tile([P, NPOS], U32, align_bytes=64)
         x1_scales = keep.tile([P, NPOS], U8, align_bytes=64)
 
-        centre_of = {}
+        vector_products_of = {}
         logits_t_of = {}
         neg_max_of = {}
         gain_of = {}
@@ -148,79 +174,51 @@ def tile_lablock_kernel(tc, x, w, conv_w, conv_b, out):
         inv_total_of = {}
         gain_c_of = {}
 
-        def classes_of(index):
-            return [
-                (r, q)
-                for r in range(KT)
-                for q in range(KT)
-                if index * P <= class_start(r, q) < (index + 1) * P
-            ]
-
         def multiply_on_scalar(index):
-            centre = work.tile([P, MAX_CLASSES, CB, class_size(0)], F32, tag="centre")
-            for slot, (r, q) in enumerate(classes_of(index)):
+            for r, q in classes_of(index):
                 size = class_size(r)
                 start = class_start(r, q)
-                start2 = class_start(r, (q + 1) % KT) + (q + 1) // KT
-                for t in range(CB):
-                    nc.scalar.activation(
-                        out=centre[:, slot, t, 0:size],
-                        in_=x_cls[:, t, start : start + size],
-                        func=ACT.Copy,
-                        scale=w_f32[:, CENTRE * CB + t, r * KT + q : r * KT + q + 1],
-                    )
-                    nc.scalar.activation(
-                        out=side[:, t, start : start + size],
-                        in_=x_cls[:, t, start2 : start2 + size],
-                        func=ACT.Copy,
-                        scale=w_f32[:, SIDE * CB + t, r * KT + q : r * KT + q + 1],
-                    )
-            centre_of[index] = centre
-
-        def add_taps(index):
-            centre = centre_of[index]
-            for tap in VECTOR_TAPS:
-                di, dj = OFFSETS[tap]
-                for slot, (r, q) in enumerate(classes_of(index)):
-                    size = class_size(r)
-                    r2, a_shift = (r + di) % KT, (r + di) // KT
-                    q2, k_shift = (q + dj) % KT, (q + dj) // KT
-                    a_lo = max(0, -a_shift)
-                    a_cnt = min(rows_of(r), rows_of(r2) - a_shift) - a_lo
-                    start = class_start(r, q)
-                    start2 = class_start(r2, q2) + k_shift
+                for slot, tap in enumerate(SCALAR_TAPS):
+                    source = source_start(r, q, tap)
                     for t in range(CB):
-                        acc = main[:, t, start : start + size].rearrange("p (b z) -> p b z", b=B)[
-                            :, :, a_lo * KCOLS : (a_lo + a_cnt) * KCOLS
-                        ]
-                        moved = x_cls[:, t, start2 : start2 + class_size(r2)].rearrange(
-                            "p (b z) -> p b z", b=B
-                        )[:, :, (a_lo + a_shift) * KCOLS : (a_lo + a_shift + a_cnt) * KCOLS]
-                        if tap == VECTOR_TAPS[0]:
-                            before = centre[:, slot, t, 0:size].rearrange("p (b z) -> p b z", b=B)
-                        else:
-                            before = acc
-                        nc.vector.scalar_tensor_tensor(
-                            out=acc,
-                            in0=moved,
-                            scalar=w_f32[:, tap * CB + t, r * KT + q : r * KT + q + 1],
-                            in1=before,
-                            op0=ALU.mult,
-                            op1=ALU.add,
+                        nc.scalar.activation(
+                            out=scalar_products[:, slot, t, start : start + size],
+                            in_=x_cls[:, t, source : source + size],
+                            func=ACT.Copy,
+                            scale=w_f32[:, tap * CB + t, r * KT + q : r * KT + q + 1],
                         )
+
+        def multiply_on_vector(index):
+            products = work.tile([P, len(VECTOR_TAPS), CB, P], F32, tag="vector_products")
+            for slot, tap in enumerate(VECTOR_TAPS):
+                for r, q, first, count in pieces_of(index):
+                    column = class_start(r, q) + first - index * P
+                    source = source_start(r, q, tap) + first
+                    nc.vector.tensor_tensor(
+                        out=products[:, slot, :, column : column + count],
+                        in0=x_cls[:, :, source : source + count],
+                        in1=w_f32[:, tap * CB : (tap + 1) * CB, r * KT + q : r * KT + q + 1].to_broadcast(
+                            [P, CB, count]
+                        ),
+                        op=ALU.mult,
+                    )
+            vector_products_of[index] = products
 
         def turn_logits(index):
             cols = slice(index * P, (index + 1) * P)
             logits_t = psum_turn.tile([P, CB, P], F32, tag="logits_t")
             for t in range(CB):
-                nc.tensor.matmul(
-                    out=logits_t[:, t, :], lhsT=main[:, t, cols], rhs=ident_f32[:],
-                    is_transpose=True, start=True, stop=False,
-                )
-                nc.tensor.matmul(
-                    out=logits_t[:, t, :], lhsT=side[:, t, cols], rhs=ident_f32[:],
-                    is_transpose=True, start=False, stop=True,
-                )
+                terms = [scalar_products[:, slot, t, cols] for slot in range(len(SCALAR_TAPS))]
+                terms.extend(vector_products_of[index][:, slot, t, :] for slot in range(len(VECTOR_TAPS)))
+                for n, term in enumerate(terms):
+                    nc.tensor.matmul(
+                        out=logits_t[:, t, :],
+                        lhsT=term,
+                        rhs=ident_f32[:],
+                        is_transpose=True,
+                        start=(n == 0),
+                        stop=(n == len(terms) - 1),
+                    )
             logits_t_of[index] = logits_t
 
         def find_max(index):
@@ -255,13 +253,8 @@ def tile_lablock_kernel(tc, x, w, conv_w, conv_b, out):
 
         def make_gain(index):
             gain = gain_of[index]
-            nc.vector.tensor_scalar(
-                out=gain[:],
-                in0=gain[:],
-                scalar1=inv_total_of[index][:, 0:1],
-                scalar2=1.0,
-                op0=ALU.mult,
-                op1=ALU.add,
+            nc.scalar.activation(
+                out=gain[:], in_=gain[:], func=ACT.Identity, bias=1.0, scale=inv_total_of[index][:, 0:1]
             )
 
         def turn_gain(index):
@@ -271,22 +264,22 @@ def tile_lablock_kernel(tc, x, w, conv_w, conv_b, out):
             gain_c_of[index] = gain_c
 
         def make_x1(index):
+            x1_grouped = work.tile([P, P, CB], BF16, tag="x1_grouped", align_bytes=64)
+            for r, q, first, count in pieces_of(index):
+                column = class_start(r, q) + first - index * P
+                source = source_start(r, q, 0) + first
+                nc.vector.tensor_tensor(
+                    out=x1_grouped[:, column : column + count, :],
+                    in0=gain_c_of[index][:, :, column : column + count].rearrange("p t s -> p s t"),
+                    in1=x_cls[:, :, source : source + count].rearrange("p t s -> p s t"),
+                    op=ALU.mult,
+                )
             cols = slice(index * P, (index + 1) * P)
-            nc.vector.tensor_tensor(
-                out=x1_grouped[:, cols, :],
-                in0=gain_c_of[index][:].rearrange("p t s -> p s t"),
-                in1=x_cls[:, :, cols].rearrange("p t s -> p s t"),
-                op=ALU.mult,
-            )
             nc.vector.quantize_mx(
                 out=x1_codes[:, cols].bitcast(FP8X4),
                 scales=x1_scales[:, cols],
-                in_=x1_grouped[:, cols, :].rearrange("p s t -> p (s t)"),
+                in_=x1_grouped[:].rearrange("p s t -> p (s t)"),
             )
-
-        def window_start(r):
-            end = -(-group_start(r + 1) // ALIGN) * ALIGN
-            return max(0, end - MX_N)
 
         def convolve(r, vector_helps):
             na = rows_of(r)
@@ -304,7 +297,7 @@ def tile_lablock_kernel(tc, x, w, conv_w, conv_b, out):
                     stop=True,
                 )
                 by_class = conv[:, inside : inside + KT * class_size(r)].rearrange(
-                    "p (q b a k) -> p b a k q", q=KT, b=B, a=na
+                    "p (q a b k) -> p b a k q", q=KT, a=na, b=B
                 )
                 for b in range(B):
                     rows = stores.tile([P, rows_of(0), WPAD], F32, tag="rows")
@@ -338,7 +331,7 @@ def tile_lablock_kernel(tc, x, w, conv_w, conv_b, out):
             if running(step + 1):
                 multiply_on_scalar(step + 1)
             if running(step):
-                add_taps(step)
+                multiply_on_vector(step)
                 turn_logits(step)
             if running(step - 1):
                 find_max(step - 1)

@@ -20,18 +20,12 @@ OB = O // P
 IMG = H * W
 KCOLS = (W + KT - 1) // KT
 WPAD = KCOLS * KT
-ROW = B * KCOLS
-NPOS = H * KT * ROW
-NTILES = NPOS // P
-SRC_ROWS = (H + KT - 1) // KT + 2
-SRC_CLASS = SRC_ROWS * ROW
-SRC_COLS = -(-KT * KT * SRC_CLASS // 16) * 16
-XROOM = (H + KT - 1) * W
 MX_N = 512
 ALIGN = 64
 
 OFFSETS = ((0, 0), (-1, 0), (1, 0), (0, -1), (0, 1))
-SCALAR_TAPS = (0, 4)
+CENTRE = 0
+SIDE = 4
 VECTOR_TAPS = (3, 1, 2)
 
 FLOPS = 2 * B * IMG * C * O
@@ -42,7 +36,7 @@ def rows_of(r):
 
 
 def class_size(r):
-    return rows_of(r) * ROW
+    return B * rows_of(r) * KCOLS
 
 
 def group_start(r):
@@ -53,33 +47,10 @@ def class_start(r, q):
     return group_start(r) + q * class_size(r)
 
 
-def source_start(r, q, tap):
-    di, dj = OFFSETS[tap]
-    r2, a_shift = (r + di) % KT, (r + di) // KT
-    q2, k_shift = (q + dj) % KT, (q + dj) // KT
-    return (r2 * KT + q2) * SRC_CLASS + (1 + a_shift) * ROW + k_shift
-
-
-def classes_of(index):
-    return [
-        (r, q) for r in range(KT) for q in range(KT) if index * P <= class_start(r, q) < (index + 1) * P
-    ]
-
-
-def pieces_of(index):
-    pieces = []
-    for r in range(KT):
-        for q in range(KT):
-            lo = max(class_start(r, q), index * P)
-            hi = min(class_start(r, q) + class_size(r), (index + 1) * P)
-            if lo < hi:
-                pieces.append((r, q, lo - class_start(r, q), hi - lo))
-    return pieces
-
-
-def window_start(r):
-    end = -(-group_start(r + 1) // ALIGN) * ALIGN
-    return max(0, end - MX_N)
+NPOS = B * H * WPAD
+NTILES = NPOS // P
+MAX_CLASSES = 3
+XROOM = (H + KT - 1) * W
 
 
 def tile_lablock_kernel(tc, x, w, conv_w, conv_b, out):
@@ -88,7 +59,7 @@ def tile_lablock_kernel(tc, x, w, conv_w, conv_b, out):
         keep = ctx.enter_context(tc.tile_pool(name="keep", bufs=1))
         work = ctx.enter_context(tc.tile_pool(name="work", bufs=3))
         small = ctx.enter_context(tc.tile_pool(name="small", bufs=4))
-        stores = ctx.enter_context(tc.tile_pool(name="stores", bufs=6))
+        stores = ctx.enter_context(tc.tile_pool(name="stores", bufs=16))
         psum_setup = ctx.enter_context(tc.psum_pool(name="psum_setup", bufs=1))
         psum_turn = ctx.enter_context(tc.psum_pool(name="psum_turn", bufs=2))
         psum_conv = ctx.enter_context(tc.psum_pool(name="psum_conv", bufs=3))
@@ -112,30 +83,8 @@ def tile_lablock_kernel(tc, x, w, conv_w, conv_b, out):
         ident_bf = keep.tile([P, P], BF16)
         make_identity(nc, ident_bf[:])
 
-        x_cls = keep.tile([P, CB, SRC_COLS], BF16)
-        full_q = W - (KCOLS - 1) * KT
-        for t in range(CB):
-            nc.vector.memset(x_cls[:, t, :].bitcast(I32), 0)
-            for r in range(KT):
-                na = rows_of(r)
-                for b in range(B):
-                    src = (
-                        x_img[:, t, b, r * W : r * W + KT * W * na]
-                        .rearrange("p (a z) -> p a z", z=KT * W)[:, :, 0:WPAD]
-                        .rearrange("p a (k q) -> p q a k", q=KT)
-                    )
-                    dst = x_cls[:, t, r * KT * SRC_CLASS : (r + 1) * KT * SRC_CLASS].rearrange(
-                        "p (q a b k) -> p q a b k", q=KT, a=SRC_ROWS, b=B
-                    )[:, :, 1 : 1 + na, b, :]
-                    pieces = (
-                        (dst[:, 0:full_q], src[:, 0:full_q]),
-                        (dst[:, full_q:KT, :, 0 : KCOLS - 1], src[:, full_q:KT, :, 0 : KCOLS - 1]),
-                    )
-                    for piece_out, piece_in in pieces:
-                        if t % 2 == 0:
-                            nc.vector.tensor_copy(out=piece_out, in_=piece_in)
-                        else:
-                            nc.scalar.copy(out=piece_out, in_=piece_in)
+        x_cls = keep.tile([P, CB, NPOS], BF16)
+        nc.vector.memset(x_cls[:].bitcast(I32), 0)
 
         w_f32 = keep.tile([P, len(OFFSETS) * CB, KT * KT], F32)
         nc.vector.tensor_copy(out=w_f32[:], in_=w_bf[:])
@@ -162,11 +111,36 @@ def tile_lablock_kernel(tc, x, w, conv_w, conv_b, out):
         bias = keep.tile([P, OB], F32)
         nc.vector.tensor_copy(out=bias[:], in_=bias_turned[:, 0, 0:OB])
 
-        scalar_products = keep.tile([P, len(SCALAR_TAPS), CB, NPOS], F32)
+        for t in range(CB):
+            for r in range(KT):
+                na = rows_of(r)
+                for b in range(B):
+                    src = (
+                        x_img[:, t, b, r * W : r * W + KT * W * na]
+                        .rearrange("p (a z) -> p a z", z=KT * W)[:, :, 0:WPAD]
+                        .rearrange("p a (k q) -> p q a k", q=KT)
+                    )
+                    dst = x_cls[:, t, group_start(r) : group_start(r + 1)].rearrange(
+                        "p (q b a k) -> p q b a k", q=KT, b=B, a=na
+                    )[:, :, b]
+                    full_q = W - (KCOLS - 1) * KT
+                    pieces = (
+                        (dst[:, 0:full_q], src[:, 0:full_q]),
+                        (dst[:, full_q:KT, :, 0 : KCOLS - 1], src[:, full_q:KT, :, 0 : KCOLS - 1]),
+                    )
+                    for piece_out, piece_in in pieces:
+                        if t % 2 == 0:
+                            nc.vector.tensor_copy(out=piece_out, in_=piece_in)
+                        else:
+                            nc.scalar.copy(out=piece_out, in_=piece_in)
+
+        main = keep.tile([P, CB, NPOS], F32)
+        side = keep.tile([P, CB, NPOS], F32)
+        x1_grouped = keep.tile([P, NPOS, CB], BF16, align_bytes=64)
         x1_codes = keep.tile([P, NPOS], U32, align_bytes=64)
         x1_scales = keep.tile([P, NPOS], U8, align_bytes=64)
 
-        vector_products_of = {}
+        centre_of = {}
         logits_t_of = {}
         neg_max_of = {}
         gain_of = {}
@@ -174,51 +148,79 @@ def tile_lablock_kernel(tc, x, w, conv_w, conv_b, out):
         inv_total_of = {}
         gain_c_of = {}
 
+        def classes_of(index):
+            return [
+                (r, q)
+                for r in range(KT)
+                for q in range(KT)
+                if index * P <= class_start(r, q) < (index + 1) * P
+            ]
+
         def multiply_on_scalar(index):
-            for r, q in classes_of(index):
+            centre = work.tile([P, MAX_CLASSES, CB, class_size(0)], F32, tag="centre")
+            for slot, (r, q) in enumerate(classes_of(index)):
                 size = class_size(r)
                 start = class_start(r, q)
-                for slot, tap in enumerate(SCALAR_TAPS):
-                    source = source_start(r, q, tap)
-                    for t in range(CB):
-                        nc.scalar.activation(
-                            out=scalar_products[:, slot, t, start : start + size],
-                            in_=x_cls[:, t, source : source + size],
-                            func=ACT.Copy,
-                            scale=w_f32[:, tap * CB + t, r * KT + q : r * KT + q + 1],
-                        )
-
-        def multiply_on_vector(index):
-            products = work.tile([P, len(VECTOR_TAPS), CB, P], F32, tag="vector_products")
-            for slot, tap in enumerate(VECTOR_TAPS):
-                for r, q, first, count in pieces_of(index):
-                    column = class_start(r, q) + first - index * P
-                    source = source_start(r, q, tap) + first
-                    nc.vector.tensor_tensor(
-                        out=products[:, slot, :, column : column + count],
-                        in0=x_cls[:, :, source : source + count],
-                        in1=w_f32[:, tap * CB : (tap + 1) * CB, r * KT + q : r * KT + q + 1].to_broadcast(
-                            [P, CB, count]
-                        ),
-                        op=ALU.mult,
+                start2 = class_start(r, (q + 1) % KT) + (q + 1) // KT
+                for t in range(CB):
+                    nc.scalar.activation(
+                        out=centre[:, slot, t, 0:size],
+                        in_=x_cls[:, t, start : start + size],
+                        func=ACT.Copy,
+                        scale=w_f32[:, CENTRE * CB + t, r * KT + q : r * KT + q + 1],
                     )
-            vector_products_of[index] = products
+                    nc.scalar.activation(
+                        out=side[:, t, start : start + size],
+                        in_=x_cls[:, t, start2 : start2 + size],
+                        func=ACT.Copy,
+                        scale=w_f32[:, SIDE * CB + t, r * KT + q : r * KT + q + 1],
+                    )
+            centre_of[index] = centre
+
+        def add_taps(index):
+            centre = centre_of[index]
+            for tap in VECTOR_TAPS:
+                di, dj = OFFSETS[tap]
+                for slot, (r, q) in enumerate(classes_of(index)):
+                    size = class_size(r)
+                    r2, a_shift = (r + di) % KT, (r + di) // KT
+                    q2, k_shift = (q + dj) % KT, (q + dj) // KT
+                    a_lo = max(0, -a_shift)
+                    a_cnt = min(rows_of(r), rows_of(r2) - a_shift) - a_lo
+                    start = class_start(r, q)
+                    start2 = class_start(r2, q2) + k_shift
+                    for t in range(CB):
+                        acc = main[:, t, start : start + size].rearrange("p (b z) -> p b z", b=B)[
+                            :, :, a_lo * KCOLS : (a_lo + a_cnt) * KCOLS
+                        ]
+                        moved = x_cls[:, t, start2 : start2 + class_size(r2)].rearrange(
+                            "p (b z) -> p b z", b=B
+                        )[:, :, (a_lo + a_shift) * KCOLS : (a_lo + a_shift + a_cnt) * KCOLS]
+                        if tap == VECTOR_TAPS[0]:
+                            before = centre[:, slot, t, 0:size].rearrange("p (b z) -> p b z", b=B)
+                        else:
+                            before = acc
+                        nc.vector.scalar_tensor_tensor(
+                            out=acc,
+                            in0=moved,
+                            scalar=w_f32[:, tap * CB + t, r * KT + q : r * KT + q + 1],
+                            in1=before,
+                            op0=ALU.mult,
+                            op1=ALU.add,
+                        )
 
         def turn_logits(index):
             cols = slice(index * P, (index + 1) * P)
             logits_t = psum_turn.tile([P, CB, P], F32, tag="logits_t")
             for t in range(CB):
-                terms = [scalar_products[:, slot, t, cols] for slot in range(len(SCALAR_TAPS))]
-                terms.extend(vector_products_of[index][:, slot, t, :] for slot in range(len(VECTOR_TAPS)))
-                for n, term in enumerate(terms):
-                    nc.tensor.matmul(
-                        out=logits_t[:, t, :],
-                        lhsT=term,
-                        rhs=ident_f32[:],
-                        is_transpose=True,
-                        start=(n == 0),
-                        stop=(n == len(terms) - 1),
-                    )
+                nc.tensor.matmul(
+                    out=logits_t[:, t, :], lhsT=main[:, t, cols], rhs=ident_f32[:],
+                    is_transpose=True, start=True, stop=False,
+                )
+                nc.tensor.matmul(
+                    out=logits_t[:, t, :], lhsT=side[:, t, cols], rhs=ident_f32[:],
+                    is_transpose=True, start=False, stop=True,
+                )
             logits_t_of[index] = logits_t
 
         def find_max(index):
@@ -264,22 +266,22 @@ def tile_lablock_kernel(tc, x, w, conv_w, conv_b, out):
             gain_c_of[index] = gain_c
 
         def make_x1(index):
-            x1_grouped = work.tile([P, P, CB], BF16, tag="x1_grouped", align_bytes=64)
-            for r, q, first, count in pieces_of(index):
-                column = class_start(r, q) + first - index * P
-                source = source_start(r, q, 0) + first
-                nc.vector.tensor_tensor(
-                    out=x1_grouped[:, column : column + count, :],
-                    in0=gain_c_of[index][:, :, column : column + count].rearrange("p t s -> p s t"),
-                    in1=x_cls[:, :, source : source + count].rearrange("p t s -> p s t"),
-                    op=ALU.mult,
-                )
             cols = slice(index * P, (index + 1) * P)
+            nc.vector.tensor_tensor(
+                out=x1_grouped[:, cols, :],
+                in0=gain_c_of[index][:].rearrange("p t s -> p s t"),
+                in1=x_cls[:, :, cols].rearrange("p t s -> p s t"),
+                op=ALU.mult,
+            )
             nc.vector.quantize_mx(
                 out=x1_codes[:, cols].bitcast(FP8X4),
                 scales=x1_scales[:, cols],
-                in_=x1_grouped[:].rearrange("p s t -> p (s t)"),
+                in_=x1_grouped[:, cols, :].rearrange("p s t -> p (s t)"),
             )
+
+        def window_start(r):
+            end = -(-group_start(r + 1) // ALIGN) * ALIGN
+            return max(0, end - MX_N)
 
         def convolve(r, vector_helps):
             na = rows_of(r)
@@ -297,7 +299,7 @@ def tile_lablock_kernel(tc, x, w, conv_w, conv_b, out):
                     stop=True,
                 )
                 by_class = conv[:, inside : inside + KT * class_size(r)].rearrange(
-                    "p (q a b k) -> p b a k q", q=KT, a=na, b=B
+                    "p (q b a k) -> p b a k q", q=KT, b=B, a=na
                 )
                 for b in range(B):
                     rows = stores.tile([P, rows_of(0), WPAD], F32, tag="rows")
@@ -331,7 +333,7 @@ def tile_lablock_kernel(tc, x, w, conv_w, conv_b, out):
             if running(step + 1):
                 multiply_on_scalar(step + 1)
             if running(step):
-                multiply_on_vector(step)
+                add_taps(step)
                 turn_logits(step)
             if running(step - 1):
                 find_max(step - 1)

@@ -49,6 +49,8 @@ def class_start(r, q):
 
 NPOS = B * H * WPAD
 NTILES = NPOS // P
+SCALAR_LEAD = 2
+CONV_PER_STEP = 2
 MAX_CLASSES = 3
 XROOM = (H + KT - 1) * W
 
@@ -57,12 +59,13 @@ def tile_lablock_kernel(tc, x, w, conv_w, conv_b, out):
     nc = tc.nc
     with ExitStack() as ctx:
         keep = ctx.enter_context(tc.tile_pool(name="keep", bufs=1))
-        work = ctx.enter_context(tc.tile_pool(name="work", bufs=3))
+        work = ctx.enter_context(tc.tile_pool(name="work", bufs=4))
         small = ctx.enter_context(tc.tile_pool(name="small", bufs=4))
         stores = ctx.enter_context(tc.tile_pool(name="stores", bufs=16))
         psum_setup = ctx.enter_context(tc.psum_pool(name="psum_setup", bufs=1))
         psum_turn = ctx.enter_context(tc.psum_pool(name="psum_turn", bufs=2))
         psum_conv = ctx.enter_context(tc.psum_pool(name="psum_conv", bufs=3))
+        ctx.enter_context(tc.manual_schedule())
 
         x_img = keep.tile([P, CB, B, XROOM], BF16)
         for t in range(CB):
@@ -87,33 +90,21 @@ def tile_lablock_kernel(tc, x, w, conv_w, conv_b, out):
         nc.vector.memset(x_cls[:].bitcast(I32), 0)
 
         w_f32 = keep.tile([P, len(OFFSETS) * CB, KT * KT], F32)
-        nc.vector.tensor_copy(out=w_f32[:], in_=w_bf[:])
 
-        cw_grouped = keep.tile([P, O, CB], BF16, align_bytes=64)
-        for ob in range(OB):
-            cw_turned = psum_setup.tile([P, CB, P], BF16, tag="setup")
+        def classes_of(index):
+            return [
+                (r, q)
+                for r in range(KT)
+                for q in range(KT)
+                if index * P <= class_start(r, q) < (index + 1) * P
+            ]
+
+        rows_sorted = set()
+
+        def sort_rows(r):
+            na = rows_of(r)
+            full_q = W - (KCOLS - 1) * KT
             for t in range(CB):
-                nc.tensor.transpose(cw_turned[:, t, :], cw_rows[:, ob, t * P : (t + 1) * P], ident_bf[:])
-            nc.vector.tensor_copy(
-                out=cw_grouped[:, ob * P : (ob + 1) * P, :],
-                in_=cw_turned[:].rearrange("p t o -> p o t"),
-            )
-        cw_codes = keep.tile([P, O], U32, align_bytes=64)
-        cw_scales = keep.tile([P, O], U8, align_bytes=64)
-        nc.vector.quantize_mx(
-            out=cw_codes[:].bitcast(FP8X4),
-            scales=cw_scales[:],
-            in_=cw_grouped[:].rearrange("p o t -> p (o t)"),
-        )
-
-        bias_turned = psum_setup.tile([P, CB, P], BF16, tag="setup")
-        nc.tensor.transpose(bias_turned[:, 0, :], bias_rows[:], ident_bf[:])
-        bias = keep.tile([P, OB], F32)
-        nc.vector.tensor_copy(out=bias[:], in_=bias_turned[:, 0, 0:OB])
-
-        for t in range(CB):
-            for r in range(KT):
-                na = rows_of(r)
                 for b in range(B):
                     src = (
                         x_img[:, t, b, r * W : r * W + KT * W * na]
@@ -123,7 +114,6 @@ def tile_lablock_kernel(tc, x, w, conv_w, conv_b, out):
                     dst = x_cls[:, t, group_start(r) : group_start(r + 1)].rearrange(
                         "p (q b a k) -> p q b a k", q=KT, b=B, a=na
                     )[:, :, b]
-                    full_q = W - (KCOLS - 1) * KT
                     pieces = (
                         (dst[:, 0:full_q], src[:, 0:full_q]),
                         (dst[:, full_q:KT, :, 0 : KCOLS - 1], src[:, full_q:KT, :, 0 : KCOLS - 1]),
@@ -133,6 +123,13 @@ def tile_lablock_kernel(tc, x, w, conv_w, conv_b, out):
                             nc.vector.tensor_copy(out=piece_out, in_=piece_in)
                         else:
                             nc.scalar.copy(out=piece_out, in_=piece_in)
+            rows_sorted.add(r)
+
+        def sort_rows_for(index):
+            for r, q in classes_of(index):
+                for r_read in ((r - 1) % KT, r, (r + 1) % KT):
+                    if r_read not in rows_sorted:
+                        sort_rows(r_read)
 
         main = keep.tile([P, CB, NPOS], F32)
         side = keep.tile([P, CB, NPOS], F32)
@@ -147,14 +144,7 @@ def tile_lablock_kernel(tc, x, w, conv_w, conv_b, out):
         total_of = {}
         inv_total_of = {}
         gain_c_of = {}
-
-        def classes_of(index):
-            return [
-                (r, q)
-                for r in range(KT)
-                for q in range(KT)
-                if index * P <= class_start(r, q) < (index + 1) * P
-            ]
+        conv_of = {}
 
         def multiply_on_scalar(index):
             centre = work.tile([P, MAX_CLASSES, CB, class_size(0)], F32, tag="centre")
@@ -283,55 +273,91 @@ def tile_lablock_kernel(tc, x, w, conv_w, conv_b, out):
             end = -(-group_start(r + 1) // ALIGN) * ALIGN
             return max(0, end - MX_N)
 
-        def convolve(r, vector_helps):
-            na = rows_of(r)
+        def convolve(r, ob):
             first = window_start(r)
-            inside = group_start(r) - first
-            for ob in range(OB):
-                conv = psum_conv.tile([P, MX_N], F32, tag="conv")
-                nc.tensor.matmul_mx(
-                    out=conv[:],
-                    lhsT=cw_codes[:, ob * P : (ob + 1) * P].bitcast(FP8X4),
-                    lhsT_scale=cw_scales[:, ob * P : (ob + 1) * P],
-                    rhs=x1_codes[:, first : first + MX_N].bitcast(FP8X4),
-                    rhs_scale=x1_scales[:, first : first + MX_N],
-                    start=True,
-                    stop=True,
-                )
-                by_class = conv[:, inside : inside + KT * class_size(r)].rearrange(
-                    "p (q b a k) -> p b a k q", q=KT, b=B, a=na
-                )
-                for b in range(B):
-                    rows = stores.tile([P, rows_of(0), WPAD], F32, tag="rows")
-                    in_order = rows[:, 0:na, :].rearrange("p a (k q) -> p a k q", q=KT)
-                    if vector_helps and ob % 2 == 1:
-                        nc.vector.tensor_scalar(
-                            out=in_order,
-                            in0=by_class[:, b],
-                            scalar1=bias[:, ob : ob + 1],
-                            scalar2=None,
-                            op0=ALU.add,
-                        )
-                    else:
-                        nc.scalar.activation(
-                            out=in_order,
-                            in_=by_class[:, b],
-                            func=ACT.Identity,
-                            bias=bias[:, ob : ob + 1],
-                            scale=1.0,
-                        )
-                    nc.sync.dma_start(
-                        out=out[b, ob * P : (ob + 1) * P, r:H:KT, :], in_=rows[:, 0:na, 0:W]
+            conv = psum_conv.tile([P, MX_N], F32, tag="conv")
+            nc.tensor.matmul_mx(
+                out=conv[:],
+                lhsT=cw_codes[:, ob * P : (ob + 1) * P].bitcast(FP8X4),
+                lhsT_scale=cw_scales[:, ob * P : (ob + 1) * P],
+                rhs=x1_codes[:, first : first + MX_N].bitcast(FP8X4),
+                rhs_scale=x1_scales[:, first : first + MX_N],
+                start=True,
+                stop=True,
+            )
+            conv_of[(r, ob)] = conv
+
+        def store(r, ob, on_vector):
+            na = rows_of(r)
+            inside = group_start(r) - window_start(r)
+            by_class = conv_of[(r, ob)][:, inside : inside + KT * class_size(r)].rearrange(
+                "p (q b a k) -> p b a k q", q=KT, b=B, a=na
+            )
+            for b in range(B):
+                rows = stores.tile([P, rows_of(0), WPAD], F32, tag="rows")
+                in_order = rows[:, 0:na, :].rearrange("p a (k q) -> p a k q", q=KT)
+                if on_vector:
+                    nc.vector.tensor_scalar(
+                        out=in_order,
+                        in0=by_class[:, b],
+                        scalar1=bias[:, ob : ob + 1],
+                        scalar2=None,
+                        op0=ALU.add,
                     )
+                else:
+                    nc.scalar.activation(
+                        out=in_order,
+                        in_=by_class[:, b],
+                        func=ACT.Identity,
+                        bias=bias[:, ob : ob + 1],
+                        scale=1.0,
+                    )
+                nc.sync.dma_start(out=out[b, ob * P : (ob + 1) * P, r:H:KT, :], in_=rows[:, 0:na, 0:W])
+
+        cw_codes = keep.tile([P, O], U32, align_bytes=64)
+        cw_scales = keep.tile([P, O], U8, align_bytes=64)
+        bias = keep.tile([P, OB], F32)
+
+        def prepare_conv_w():
+            cw_grouped = keep.tile([P, O, CB], BF16, align_bytes=64)
+            for ob in range(OB):
+                cw_turned = psum_setup.tile([P, CB, P], BF16, tag="setup")
+                for t in range(CB):
+                    nc.tensor.transpose(cw_turned[:, t, :], cw_rows[:, ob, t * P : (t + 1) * P], ident_bf[:])
+                nc.vector.tensor_copy(
+                    out=cw_grouped[:, ob * P : (ob + 1) * P, :],
+                    in_=cw_turned[:].rearrange("p t o -> p o t"),
+                )
+            nc.vector.quantize_mx(
+                out=cw_codes[:].bitcast(FP8X4),
+                scales=cw_scales[:],
+                in_=cw_grouped[:].rearrange("p o t -> p (o t)"),
+            )
+            bias_turned = psum_setup.tile([P, CB, P], BF16, tag="setup")
+            nc.tensor.transpose(bias_turned[:, 0, :], bias_rows[:], ident_bf[:])
+            nc.vector.tensor_copy(out=bias[:], in_=bias_turned[:, 0, 0:OB])
 
         def running(index):
             return 0 <= index < NTILES
 
-        groups_done = 0
-        multiply_on_scalar(0)
+        sort_rows_for(0)
+        nc.vector.tensor_copy(out=w_f32[:], in_=w_bf[:])
+        for index in range(SCALAR_LEAD):
+            sort_rows_for(index)
+            multiply_on_scalar(index)
+        prepare_conv_w()
+        groups_seen = 0
+        waiting = []
         for step in range(NTILES + 3):
-            if running(step + 1):
-                multiply_on_scalar(step + 1)
+            blocks = waiting[0:CONV_PER_STEP]
+            waiting = waiting[CONV_PER_STEP:]
+            for r, ob in blocks:
+                convolve(r, ob)
+            if running(step + SCALAR_LEAD):
+                sort_rows_for(step + SCALAR_LEAD)
+                multiply_on_scalar(step + SCALAR_LEAD)
+            for r, ob in blocks:
+                store(r, ob, on_vector=False)
             if running(step):
                 add_taps(step)
                 turn_logits(step)
@@ -344,6 +370,9 @@ def tile_lablock_kernel(tc, x, w, conv_w, conv_b, out):
                 turn_gain(step - 2)
             if running(step - 3):
                 make_x1(step - 3)
-            while groups_done < KT and window_start(groups_done) + MX_N <= (step - 2) * P:
-                convolve(groups_done, vector_helps=step >= NTILES)
-                groups_done += 1
+            while groups_seen < KT and window_start(groups_seen) + MX_N <= (step - 2) * P:
+                waiting.extend((groups_seen, ob) for ob in range(OB))
+                groups_seen += 1
+        for r, ob in waiting:
+            convolve(r, ob)
+            store(r, ob, on_vector=(ob % 2 == 1))

@@ -51,6 +51,7 @@ NPOS = B * H * WPAD
 NTILES = NPOS // P
 SCALAR_LEAD = 2
 CONV_PER_STEP = 2
+W_ROOM = 64
 MAX_CLASSES = 3
 XROOM = (H + KT - 1) * W
 
@@ -65,7 +66,6 @@ def tile_lablock_kernel(tc, x, w, conv_w, conv_b, out):
         psum_setup = ctx.enter_context(tc.psum_pool(name="psum_setup", bufs=1))
         psum_turn = ctx.enter_context(tc.psum_pool(name="psum_turn", bufs=2))
         psum_conv = ctx.enter_context(tc.psum_pool(name="psum_conv", bufs=3))
-        ctx.enter_context(tc.manual_schedule())
 
         x_img = keep.tile([P, CB, B, XROOM], BF16)
         for t in range(CB):
@@ -73,13 +73,15 @@ def tile_lablock_kernel(tc, x, w, conv_w, conv_b, out):
                 out=x_img[:, t, :, 0:IMG],
                 in_=x[:, t * P : (t + 1) * P].rearrange("b p i j -> p b (i j)"),
             )
-        w_bf = keep.tile([P, len(OFFSETS) * CB, KT * KT], BF16)
-        nc.scalar.dma_start(out=w_bf[:], in_=w.rearrange("n (t p) r q -> p (n t) (r q)", p=P))
+        w_bf = keep.tile([P, len(OFFSETS) * CB, W_ROOM], BF16)
+        nc.scalar.dma_start(
+            out=w_bf[:, :, 0 : KT * KT], in_=w.rearrange("n (t p) r q -> p (n t) (r q)", p=P)
+        )
         cw_rows = keep.tile([P, OB, C], BF16)
-        nc.scalar.dma_start(out=cw_rows[:], in_=conv_w.rearrange("(ob p) c -> p ob c", p=P))
+        nc.sync.dma_start(out=cw_rows[:], in_=conv_w.rearrange("(ob p) c -> p ob c", p=P))
         bias_rows = keep.tile([P, P], BF16)
         nc.vector.memset(bias_rows[:], 0.0)
-        nc.scalar.dma_start(out=bias_rows[0:OB, :], in_=conv_b.rearrange("(ob p) -> ob p", p=P))
+        nc.sync.dma_start(out=bias_rows[0:OB, :], in_=conv_b.rearrange("(ob p) -> ob p", p=P))
 
         ident_f32 = keep.tile([P, P], F32)
         make_identity(nc, ident_f32[:])
@@ -324,7 +326,7 @@ def tile_lablock_kernel(tc, x, w, conv_w, conv_b, out):
                 cw_turned = psum_setup.tile([P, CB, P], BF16, tag="setup")
                 for t in range(CB):
                     nc.tensor.transpose(cw_turned[:, t, :], cw_rows[:, ob, t * P : (t + 1) * P], ident_bf[:])
-                nc.vector.tensor_copy(
+                nc.scalar.copy(
                     out=cw_grouped[:, ob * P : (ob + 1) * P, :],
                     in_=cw_turned[:].rearrange("p t o -> p o t"),
                 )
@@ -335,13 +337,13 @@ def tile_lablock_kernel(tc, x, w, conv_w, conv_b, out):
             )
             bias_turned = psum_setup.tile([P, CB, P], BF16, tag="setup")
             nc.tensor.transpose(bias_turned[:, 0, :], bias_rows[:], ident_bf[:])
-            nc.vector.tensor_copy(out=bias[:], in_=bias_turned[:, 0, 0:OB])
+            nc.scalar.copy(out=bias[:], in_=bias_turned[:, 0, 0:OB])
 
         def running(index):
             return 0 <= index < NTILES
 
         sort_rows_for(0)
-        nc.vector.tensor_copy(out=w_f32[:], in_=w_bf[:])
+        nc.scalar.copy(out=w_f32[:], in_=w_bf[:, :, 0 : KT * KT])
         for index in range(SCALAR_LEAD):
             sort_rows_for(index)
             multiply_on_scalar(index)

@@ -24,8 +24,7 @@ MX_N = 512
 ALIGN = 64
 
 OFFSETS = ((0, 0), (-1, 0), (1, 0), (0, -1), (0, 1))
-CENTRE = 0
-SIDE = 4
+SCALAR_TAPS = (0, 4)
 VECTOR_TAPS = (3, 1, 2)
 
 FLOPS = 2 * B * IMG * C * O
@@ -52,7 +51,6 @@ NTILES = NPOS // P
 SCALAR_LEAD = 2
 CONV_PER_STEP = 2
 W_ROOM = 64
-MAX_CLASSES = 3
 XROOM = (H + KT - 1) * W
 
 
@@ -60,9 +58,9 @@ def tile_lablock_kernel(tc, x, w, conv_w, conv_b, out):
     nc = tc.nc
     with ExitStack() as ctx:
         keep = ctx.enter_context(tc.tile_pool(name="keep", bufs=1))
-        work = ctx.enter_context(tc.tile_pool(name="work", bufs=4))
+        work = ctx.enter_context(tc.tile_pool(name="work", bufs=3))
         small = ctx.enter_context(tc.tile_pool(name="small", bufs=4))
-        stores = ctx.enter_context(tc.tile_pool(name="stores", bufs=16))
+        stores = ctx.enter_context(tc.tile_pool(name="stores", bufs=8))
         psum_setup = ctx.enter_context(tc.psum_pool(name="psum_setup", bufs=1))
         psum_turn = ctx.enter_context(tc.psum_pool(name="psum_turn", bufs=2))
         psum_conv = ctx.enter_context(tc.psum_pool(name="psum_conv", bufs=3))
@@ -133,13 +131,11 @@ def tile_lablock_kernel(tc, x, w, conv_w, conv_b, out):
                     if r_read not in rows_sorted:
                         sort_rows(r_read)
 
-        main = keep.tile([P, CB, NPOS], F32)
-        side = keep.tile([P, CB, NPOS], F32)
-        x1_grouped = keep.tile([P, NPOS, CB], BF16, align_bytes=64)
+        scalar_products = keep.tile([P, len(SCALAR_TAPS), CB, NPOS], F32)
+        vector_sums = keep.tile([P, CB, NPOS], F32)
         x1_codes = keep.tile([P, NPOS], U32, align_bytes=64)
         x1_scales = keep.tile([P, NPOS], U8, align_bytes=64)
 
-        centre_of = {}
         logits_t_of = {}
         neg_max_of = {}
         gain_of = {}
@@ -148,71 +144,68 @@ def tile_lablock_kernel(tc, x, w, conv_w, conv_b, out):
         gain_c_of = {}
         conv_of = {}
 
+        def neighbours(r, q, tap):
+            di, dj = OFFSETS[tap]
+            r2, a_shift = (r + di) % KT, (r + di) // KT
+            q2, k_shift = (q + dj) % KT, (q + dj) // KT
+            return r2, q2, a_shift, k_shift
+
         def multiply_on_scalar(index):
-            centre = work.tile([P, MAX_CLASSES, CB, class_size(0)], F32, tag="centre")
-            for slot, (r, q) in enumerate(classes_of(index)):
+            for r, q in classes_of(index):
                 size = class_size(r)
                 start = class_start(r, q)
-                start2 = class_start(r, (q + 1) % KT) + (q + 1) // KT
-                for t in range(CB):
-                    nc.scalar.activation(
-                        out=centre[:, slot, t, 0:size],
-                        in_=x_cls[:, t, start : start + size],
-                        func=ACT.Copy,
-                        scale=w_f32[:, CENTRE * CB + t, r * KT + q : r * KT + q + 1],
-                    )
-                    nc.scalar.activation(
-                        out=side[:, t, start : start + size],
-                        in_=x_cls[:, t, start2 : start2 + size],
-                        func=ACT.Copy,
-                        scale=w_f32[:, SIDE * CB + t, r * KT + q : r * KT + q + 1],
-                    )
-            centre_of[index] = centre
+                for slot, tap in enumerate(SCALAR_TAPS):
+                    r2, q2, a_shift, k_shift = neighbours(r, q, tap)
+                    start2 = class_start(r2, q2) + k_shift
+                    for t in range(CB):
+                        nc.scalar.activation(
+                            out=scalar_products[:, slot, t, start : start + size],
+                            in_=x_cls[:, t, start2 : start2 + size],
+                            func=ACT.Copy,
+                            scale=w_f32[:, tap * CB + t, r * KT + q : r * KT + q + 1],
+                        )
 
         def add_taps(index):
-            centre = centre_of[index]
             for tap in VECTOR_TAPS:
-                di, dj = OFFSETS[tap]
-                for slot, (r, q) in enumerate(classes_of(index)):
+                for r, q in classes_of(index):
                     size = class_size(r)
-                    r2, a_shift = (r + di) % KT, (r + di) // KT
-                    q2, k_shift = (q + dj) % KT, (q + dj) // KT
+                    r2, q2, a_shift, k_shift = neighbours(r, q, tap)
                     a_lo = max(0, -a_shift)
                     a_cnt = min(rows_of(r), rows_of(r2) - a_shift) - a_lo
                     start = class_start(r, q)
                     start2 = class_start(r2, q2) + k_shift
                     for t in range(CB):
-                        acc = main[:, t, start : start + size].rearrange("p (b z) -> p b z", b=B)[
+                        acc = vector_sums[:, t, start : start + size].rearrange("p (b z) -> p b z", b=B)[
                             :, :, a_lo * KCOLS : (a_lo + a_cnt) * KCOLS
                         ]
                         moved = x_cls[:, t, start2 : start2 + class_size(r2)].rearrange(
                             "p (b z) -> p b z", b=B
                         )[:, :, (a_lo + a_shift) * KCOLS : (a_lo + a_shift + a_cnt) * KCOLS]
+                        weight = w_f32[:, tap * CB + t, r * KT + q : r * KT + q + 1]
                         if tap == VECTOR_TAPS[0]:
-                            before = centre[:, slot, t, 0:size].rearrange("p (b z) -> p b z", b=B)
+                            nc.vector.tensor_scalar(
+                                out=acc, in0=moved, scalar1=weight, scalar2=None, op0=ALU.mult
+                            )
                         else:
-                            before = acc
-                        nc.vector.scalar_tensor_tensor(
-                            out=acc,
-                            in0=moved,
-                            scalar=w_f32[:, tap * CB + t, r * KT + q : r * KT + q + 1],
-                            in1=before,
-                            op0=ALU.mult,
-                            op1=ALU.add,
-                        )
+                            nc.vector.scalar_tensor_tensor(
+                                out=acc, in0=moved, scalar=weight, in1=acc, op0=ALU.mult, op1=ALU.add
+                            )
 
         def turn_logits(index):
             cols = slice(index * P, (index + 1) * P)
             logits_t = psum_turn.tile([P, CB, P], F32, tag="logits_t")
             for t in range(CB):
-                nc.tensor.matmul(
-                    out=logits_t[:, t, :], lhsT=main[:, t, cols], rhs=ident_f32[:],
-                    is_transpose=True, start=True, stop=False,
-                )
-                nc.tensor.matmul(
-                    out=logits_t[:, t, :], lhsT=side[:, t, cols], rhs=ident_f32[:],
-                    is_transpose=True, start=False, stop=True,
-                )
+                terms = [scalar_products[:, slot, t, cols] for slot in range(len(SCALAR_TAPS))]
+                terms.append(vector_sums[:, t, cols])
+                for n, term in enumerate(terms):
+                    nc.tensor.matmul(
+                        out=logits_t[:, t, :],
+                        lhsT=term,
+                        rhs=ident_f32[:],
+                        is_transpose=True,
+                        start=(n == 0),
+                        stop=(n == len(terms) - 1),
+                    )
             logits_t_of[index] = logits_t
 
         def find_max(index):
@@ -259,8 +252,9 @@ def tile_lablock_kernel(tc, x, w, conv_w, conv_b, out):
 
         def make_x1(index):
             cols = slice(index * P, (index + 1) * P)
+            x1_grouped = work.tile([P, P, CB], BF16, tag="x1_grouped", align_bytes=64)
             nc.vector.tensor_tensor(
-                out=x1_grouped[:, cols, :],
+                out=x1_grouped[:],
                 in0=gain_c_of[index][:].rearrange("p t s -> p s t"),
                 in1=x_cls[:, :, cols].rearrange("p t s -> p s t"),
                 op=ALU.mult,
@@ -268,7 +262,7 @@ def tile_lablock_kernel(tc, x, w, conv_w, conv_b, out):
             nc.vector.quantize_mx(
                 out=x1_codes[:, cols].bitcast(FP8X4),
                 scales=x1_scales[:, cols],
-                in_=x1_grouped[:, cols, :].rearrange("p s t -> p (s t)"),
+                in_=x1_grouped[:].rearrange("p s t -> p (s t)"),
             )
 
         def window_start(r):

from contextlib import ExitStack

import concourse.mybir as mybir
from concourse.masks import make_identity

BF16 = mybir.dt.bfloat16
F32 = mybir.dt.float32
I32 = mybir.dt.int32
U32 = mybir.dt.uint32
U8 = mybir.dt.uint8
FP8X4 = mybir.dt.float8_e4m3fn_x4
ALU = mybir.AluOpType
ACT = mybir.ActivationFunctionType
AXIS = mybir.AxisListType

P = 128
B, C, O, H, W, KT = 2, 512, 512, 32, 40, 7
CB = C // P
OB = O // P
IMG = H * W
KCOLS = (W + KT - 1) // KT
WPAD = KCOLS * KT
MX_N = 512
ALIGN = 64

OFFSETS = ((0, 0), (-1, 0), (1, 0), (0, -1), (0, 1))
SCALAR_TAPS = (0, 4)
VECTOR_TAPS = (3, 1, 2)

FLOPS = 2 * B * IMG * C * O


def rows_of(r):
    return (H - r + KT - 1) // KT


def class_size(r):
    return B * rows_of(r) * KCOLS


def group_start(r):
    return sum(KT * class_size(rr) for rr in range(r))


def class_start(r, q):
    return group_start(r) + q * class_size(r)


NPOS = B * H * WPAD
NTILES = NPOS // P
SCALAR_LEAD = 2
CONV_PER_STEP = 2
W_ROOM = 64
XROOM = (H + KT - 1) * W


def tile_lablock_kernel(tc, x, w, conv_w, conv_b, out):
    nc = tc.nc
    with ExitStack() as ctx:
        keep = ctx.enter_context(tc.tile_pool(name="keep", bufs=1))
        work = ctx.enter_context(tc.tile_pool(name="work", bufs=3))
        small = ctx.enter_context(tc.tile_pool(name="small", bufs=4))
        stores = ctx.enter_context(tc.tile_pool(name="stores", bufs=8))
        psum_setup = ctx.enter_context(tc.psum_pool(name="psum_setup", bufs=1))
        psum_turn = ctx.enter_context(tc.psum_pool(name="psum_turn", bufs=2))
        psum_conv = ctx.enter_context(tc.psum_pool(name="psum_conv", bufs=3))

        x_img = keep.tile([P, CB, B, XROOM], BF16)
        for t in range(CB):
            nc.sync.dma_start(
                out=x_img[:, t, :, 0:IMG],
                in_=x[:, t * P : (t + 1) * P].rearrange("b p i j -> p b (i j)"),
            )
        w_bf = keep.tile([P, len(OFFSETS) * CB, W_ROOM], BF16)
        nc.scalar.dma_start(
            out=w_bf[:, :, 0 : KT * KT], in_=w.rearrange("n (t p) r q -> p (n t) (r q)", p=P)
        )
        cw_rows = keep.tile([P, OB, C], BF16)
        nc.sync.dma_start(out=cw_rows[:], in_=conv_w.rearrange("(ob p) c -> p ob c", p=P))
        bias_rows = keep.tile([P, P], BF16)
        nc.vector.memset(bias_rows[:], 0.0)
        nc.sync.dma_start(out=bias_rows[0:OB, :], in_=conv_b.rearrange("(ob p) -> ob p", p=P))

        ident_f32 = keep.tile([P, P], F32)
        make_identity(nc, ident_f32[:])
        ident_bf = keep.tile([P, P], BF16)
        make_identity(nc, ident_bf[:])

        x_cls = keep.tile([P, CB, NPOS], BF16)
        nc.vector.memset(x_cls[:].bitcast(I32), 0)

        w_f32 = keep.tile([P, len(OFFSETS) * CB, KT * KT], F32)

        def classes_of(index):
            return [
                (r, q)
                for r in range(KT)
                for q in range(KT)
                if index * P <= class_start(r, q) < (index + 1) * P
            ]

        rows_sorted = set()

        def sort_rows(r):
            na = rows_of(r)
            full_q = W - (KCOLS - 1) * KT
            for t in range(CB):
                for b in range(B):
                    src = (
                        x_img[:, t, b, r * W : r * W + KT * W * na]
                        .rearrange("p (a z) -> p a z", z=KT * W)[:, :, 0:WPAD]
                        .rearrange("p a (k q) -> p q a k", q=KT)
                    )
                    dst = x_cls[:, t, group_start(r) : group_start(r + 1)].rearrange(
                        "p (q b a k) -> p q b a k", q=KT, b=B, a=na
                    )[:, :, b]
                    pieces = (
                        (dst[:, 0:full_q], src[:, 0:full_q]),
                        (dst[:, full_q:KT, :, 0 : KCOLS - 1], src[:, full_q:KT, :, 0 : KCOLS - 1]),
                    )
                    for piece_out, piece_in in pieces:
                        if t % 2 == 0:
                            nc.vector.tensor_copy(out=piece_out, in_=piece_in)
                        else:
                            nc.scalar.copy(out=piece_out, in_=piece_in)
            rows_sorted.add(r)

        def sort_rows_for(index):
            for r, q in classes_of(index):
                for r_read in ((r - 1) % KT, r, (r + 1) % KT):
                    if r_read not in rows_sorted:
                        sort_rows(r_read)

        scalar_products = keep.tile([P, len(SCALAR_TAPS), CB, NPOS], F32)
        vector_sums = keep.tile([P, CB, NPOS], F32)
        x1_codes = keep.tile([P, NPOS], U32, align_bytes=64)
        x1_scales = keep.tile([P, NPOS], U8, align_bytes=64)

        logits_t_of = {}
        neg_max_of = {}
        gain_of = {}
        total_of = {}
        inv_total_of = {}
        gain_c_of = {}
        conv_of = {}

        def neighbours(r, q, tap):
            di, dj = OFFSETS[tap]
            r2, a_shift = (r + di) % KT, (r + di) // KT
            q2, k_shift = (q + dj) % KT, (q + dj) // KT
            return r2, q2, a_shift, k_shift

        def multiply_on_scalar(index):
            for r, q in classes_of(index):
                size = class_size(r)
                start = class_start(r, q)
                for slot, tap in enumerate(SCALAR_TAPS):
                    r2, q2, a_shift, k_shift = neighbours(r, q, tap)
                    start2 = class_start(r2, q2) + k_shift
                    for t in range(CB):
                        nc.scalar.activation(
                            out=scalar_products[:, slot, t, start : start + size],
                            in_=x_cls[:, t, start2 : start2 + size],
                            func=ACT.Copy,
                            scale=w_f32[:, tap * CB + t, r * KT + q : r * KT + q + 1],
                        )

        def add_taps(index):
            for tap in VECTOR_TAPS:
                for r, q in classes_of(index):
                    size = class_size(r)
                    r2, q2, a_shift, k_shift = neighbours(r, q, tap)
                    a_lo = max(0, -a_shift)
                    a_cnt = min(rows_of(r), rows_of(r2) - a_shift) - a_lo
                    start = class_start(r, q)
                    start2 = class_start(r2, q2) + k_shift
                    for t in range(CB):
                        acc = vector_sums[:, t, start : start + size].rearrange("p (b z) -> p b z", b=B)[
                            :, :, a_lo * KCOLS : (a_lo + a_cnt) * KCOLS
                        ]
                        moved = x_cls[:, t, start2 : start2 + class_size(r2)].rearrange(
                            "p (b z) -> p b z", b=B
                        )[:, :, (a_lo + a_shift) * KCOLS : (a_lo + a_shift + a_cnt) * KCOLS]
                        weight = w_f32[:, tap * CB + t, r * KT + q : r * KT + q + 1]
                        if tap == VECTOR_TAPS[0]:
                            nc.vector.tensor_scalar(
                                out=acc, in0=moved, scalar1=weight, scalar2=None, op0=ALU.mult
                            )
                        else:
                            nc.vector.scalar_tensor_tensor(
                                out=acc, in0=moved, scalar=weight, in1=acc, op0=ALU.mult, op1=ALU.add
                            )

        def turn_logits(index):
            cols = slice(index * P, (index + 1) * P)
            logits_t = psum_turn.tile([P, CB, P], F32, tag="logits_t")
            for t in range(CB):
                terms = [scalar_products[:, slot, t, cols] for slot in range(len(SCALAR_TAPS))]
                terms.append(vector_sums[:, t, cols])
                for n, term in enumerate(terms):
                    nc.tensor.matmul(
                        out=logits_t[:, t, :],
                        lhsT=term,
                        rhs=ident_f32[:],
                        is_transpose=True,
                        start=(n == 0),
                        stop=(n == len(terms) - 1),
                    )
            logits_t_of[index] = logits_t

        def find_max(index):
            neg_max = small.tile([P, 1], F32, tag="neg_max")
            nc.vector.tensor_reduce(
                out=neg_max[:],
                in_=logits_t_of[index][:].rearrange("p t c -> p (t c)"),
                axis=AXIS.X,
                op=ALU.max,
                negate=True,
            )
            neg_max_of[index] = neg_max

        def exponentials(index):
            gain = work.tile([P, C], F32, tag="gain")
            total = small.tile([P, 1], F32, tag="total")
            nc.scalar.activation(
                out=gain[:],
                in_=logits_t_of[index][:].rearrange("p t c -> p (t c)"),
                func=ACT.Exp,
                bias=neg_max_of[index][:, 0:1],
                scale=1.0,
                accum_out=total[:, 0:1],
            )
            gain_of[index] = gain
            total_of[index] = total

        def invert_total(index):
            inv_total = small.tile([P, 1], F32, tag="inv_total")
            nc.vector.reciprocal(inv_total[:], total_of[index][:])
            inv_total_of[index] = inv_total

        def make_gain(index):
            gain = gain_of[index]
            nc.scalar.activation(
                out=gain[:], in_=gain[:], func=ACT.Identity, bias=1.0, scale=inv_total_of[index][:, 0:1]
            )

        def turn_gain(index):
            gain_c = psum_turn.tile([P, CB, P], F32, tag="gain_c")
            for t in range(CB):
                nc.tensor.transpose(gain_c[:, t, :], gain_of[index][:, t * P : (t + 1) * P], ident_f32[:])
            gain_c_of[index] = gain_c

        def make_x1(index):
            cols = slice(index * P, (index + 1) * P)
            x1_grouped = work.tile([P, P, CB], BF16, tag="x1_grouped", align_bytes=64)
            nc.vector.tensor_tensor(
                out=x1_grouped[:],
                in0=gain_c_of[index][:].rearrange("p t s -> p s t"),
                in1=x_cls[:, :, cols].rearrange("p t s -> p s t"),
                op=ALU.mult,
            )
            nc.vector.quantize_mx(
                out=x1_codes[:, cols].bitcast(FP8X4),
                scales=x1_scales[:, cols],
                in_=x1_grouped[:].rearrange("p s t -> p (s t)"),
            )

        def window_start(r):
            end = -(-group_start(r + 1) // ALIGN) * ALIGN
            return max(0, end - MX_N)

        def convolve(r, ob):
            first = window_start(r)
            conv = psum_conv.tile([P, MX_N], F32, tag="conv")
            nc.tensor.matmul_mx(
                out=conv[:],
                lhsT=cw_codes[:, ob * P : (ob + 1) * P].bitcast(FP8X4),
                lhsT_scale=cw_scales[:, ob * P : (ob + 1) * P],
                rhs=x1_codes[:, first : first + MX_N].bitcast(FP8X4),
                rhs_scale=x1_scales[:, first : first + MX_N],
                start=True,
                stop=True,
            )
            conv_of[(r, ob)] = conv

        def store(r, ob, on_vector):
            na = rows_of(r)
            inside = group_start(r) - window_start(r)
            by_class = conv_of[(r, ob)][:, inside : inside + KT * class_size(r)].rearrange(
                "p (q b a k) -> p b a k q", q=KT, b=B, a=na
            )
            for b in range(B):
                rows = stores.tile([P, rows_of(0), WPAD], F32, tag="rows")
                in_order = rows[:, 0:na, :].rearrange("p a (k q) -> p a k q", q=KT)
                if on_vector:
                    nc.vector.tensor_scalar(
                        out=in_order,
                        in0=by_class[:, b],
                        scalar1=bias[:, ob : ob + 1],
                        scalar2=None,
                        op0=ALU.add,
                    )
                else:
                    nc.scalar.activation(
                        out=in_order,
                        in_=by_class[:, b],
                        func=ACT.Identity,
                        bias=bias[:, ob : ob + 1],
                        scale=1.0,
                    )
                nc.sync.dma_start(out=out[b, ob * P : (ob + 1) * P, r:H:KT, :], in_=rows[:, 0:na, 0:W])

        cw_codes = keep.tile([P, O], U32, align_bytes=64)
        cw_scales = keep.tile([P, O], U8, align_bytes=64)
        bias = keep.tile([P, OB], F32)

        def prepare_conv_w():
            cw_grouped = keep.tile([P, O, CB], BF16, align_bytes=64)
            for ob in range(OB):
                cw_turned = psum_setup.tile([P, CB, P], BF16, tag="setup")
                for t in range(CB):
                    nc.tensor.transpose(cw_turned[:, t, :], cw_rows[:, ob, t * P : (t + 1) * P], ident_bf[:])
                nc.scalar.copy(
                    out=cw_grouped[:, ob * P : (ob + 1) * P, :],
                    in_=cw_turned[:].rearrange("p t o -> p o t"),
                )
            nc.vector.quantize_mx(
                out=cw_codes[:].bitcast(FP8X4),
                scales=cw_scales[:],
                in_=cw_grouped[:].rearrange("p o t -> p (o t)"),
            )
            bias_turned = psum_setup.tile([P, CB, P], BF16, tag="setup")
            nc.tensor.transpose(bias_turned[:, 0, :], bias_rows[:], ident_bf[:])
            nc.scalar.copy(out=bias[:], in_=bias_turned[:, 0, 0:OB])

        def running(index):
            return 0 <= index < NTILES

        sort_rows_for(0)
        nc.scalar.copy(out=w_f32[:], in_=w_bf[:, :, 0 : KT * KT])
        for index in range(SCALAR_LEAD):
            sort_rows_for(index)
            multiply_on_scalar(index)
        prepare_conv_w()
        groups_seen = 0
        waiting = []
        for step in range(NTILES + 3):
            blocks = waiting[0:CONV_PER_STEP]
            waiting = waiting[CONV_PER_STEP:]
            for r, ob in blocks:
                convolve(r, ob)
            if running(step + SCALAR_LEAD):
                sort_rows_for(step + SCALAR_LEAD)
                multiply_on_scalar(step + SCALAR_LEAD)
            for r, ob in blocks:
                store(r, ob, on_vector=False)
            if running(step):
                add_taps(step)
                turn_logits(step)
            if running(step - 1):
                find_max(step - 1)
                exponentials(step - 1)
            if running(step - 2):
                invert_total(step - 2)
                make_gain(step - 2)
                turn_gain(step - 2)
            if running(step - 3):
                make_x1(step - 3)
            while groups_seen < KT and window_start(groups_seen) + MX_N <= (step - 2) * P:
                waiting.extend((groups_seen, ob) for ob in range(OB))
                groups_seen += 1
        for r, ob in waiting:
            convolve(r, ob)
            store(r, ob, on_vector=(ob % 2 == 1))
